import numpy as np
import ml_dtypes


def mxq(x, axis, fmt="e4m3"):
    dtype, down = {"e4m3": (ml_dtypes.float8_e4m3fn, 7), "e5m2": (ml_dtypes.float8_e5m2, 14)}[fmt]
    v = np.moveaxis(np.asarray(x, np.float32).astype(ml_dtypes.bfloat16).astype(np.float64), axis, -1)
    blocks = v.reshape(v.shape[:-1] + (-1, 32))
    amax = np.abs(blocks).max(-1, keepdims=True)
    byte = np.maximum(np.where(amax > 0, np.frexp(amax)[1] - 1 + 127, 0) - down, 1)
    scale = np.exp2(byte - 127.0)
    codes = (blocks / scale).astype(np.float32).astype(dtype).astype(np.float64)
    return np.moveaxis((codes * scale).reshape(v.shape), -1, axis)


WIDE = False


def mx_kscale(k):
    if not WIDE:
        return np.ones(k)
    levels = np.array([10, -10, 5, -5, 0])
    a = np.random.permutation(np.resize(levels, k // 512 * 4)).reshape(k // 512, 4)
    idx = np.arange(k)
    return np.exp2(a[idx // 512, idx % 128 // 32])


BF16 = ml_dtypes.bfloat16


def bf(x):
    return np.asarray(x, np.float32).astype(BF16)


def f64(x):
    return np.asarray(x).astype(np.float64)


B, S, D, N = 4, 64, 2048, 2048
EPS = 1e-6
GS = 6.0 / np.sqrt(D)
LEVELS = np.array([-1.0, -0.5, 0.0, 0.5, 1.0])
PROBS = np.array([0.23, 0.17, 0.2, 0.17, 0.23])


def setup_inputs():
    s = mx_kscale(D)
    s2 = np.concatenate([s, s])
    return {"x_real": bf(np.random.standard_normal((B, S, D)) * 1.2 + 0.5),
            "x_imag": bf(np.random.standard_normal((B, S, D)) * 0.7 + 0.1),
            "qw_re": bf(np.random.choice(LEVELS, size=(N, D), p=PROBS) / s),
            "qw_im": bf(np.random.choice(LEVELS, size=(N, D), p=PROBS) / s),
            "gamma": bf((1.0 + 0.1 * np.random.standard_normal(D + D)) * GS * s2),
            "beta": bf(0.2 * np.random.standard_normal(D + D) * GS * s2),
            "s_re": bf(0.7 + 0.05 * np.random.standard_normal(1)),
            "s_im": bf(0.9 + 0.05 * np.random.standard_normal(1))}


def reference(x_real, x_imag, qw_re, qw_im, gamma, beta, s_re, s_im):
    x_cat = np.concatenate([f64(x_real), f64(x_imag)], axis=-1)
    mu = x_cat.mean(axis=-1, keepdims=True)
    var = x_cat.var(axis=-1, keepdims=True)
    norm = (x_cat - mu) * (1.0 / np.sqrt(var + EPS)) * f64(gamma) + f64(beta)
    nr = mxq(norm[..., :D], 2, "e4m3")
    ni = mxq(norm[..., D:], 2, "e4m3")
    wr = mxq(f64(qw_re), 1, "e4m3").T
    wi = mxq(f64(qw_im), 1, "e4m3").T
    y_real = (nr @ wr) - (ni @ wi)
    y_imag = (nr @ wi) + (ni @ wr)
    return y_real * f64(s_re), y_imag * f64(s_im)

@@ -1,0 +1,281 @@
+from contextlib import ExitStack
+
+import concourse.mybir as mybir
+from concourse.masks import make_identity
+
+F32 = mybir.dt.float32
+BF16 = mybir.dt.bfloat16
+U32 = mybir.dt.uint32
+U8 = mybir.dt.uint8
+FP8X4 = mybir.dt.float8_e4m3fn_x4
+ALU = mybir.AluOpType
+ACT = mybir.ActivationFunctionType
+
+P = 128
+TOKENS = 256
+TOKEN_TILES = TOKENS // P
+D = 2048
+N_OUT = 2048
+EPS = 1e-6
+
+K_PASS = 512
+PASSES = D // K_PASS
+N_CHUNK = 256
+ROUNDS = N_OUT // N_CHUNK
+CHUNKS = 2 * ROUNDS
+ACC_COLS = 512
+
+W_BUFS = 5
+LEAD = 4
+
+NR, NI, NEG_NI = 0, 1, 2
+REAL, IMAG = 0, 1
+
+FLOPS = 4 * 2 * TOKENS * D * N_OUT
+
+
+def tile_realimagfourvallinear_pa_kernel(
+    tc, x_real, x_imag, qw_re, qw_im, gamma, beta, s_re, s_im, out_0, out_1
+):
+    nc = tc.nc
+    x_streams = (x_real.flatten_outer_dims(), x_imag.flatten_outer_dims())
+    weights = (qw_re, qw_im)
+    outs = (out_0.flatten_outer_dims(), out_1.flatten_outer_dims())
+
+    with ExitStack() as ctx:
+        const = ctx.enter_context(tc.tile_pool(name="const", bufs=1))
+        keep = ctx.enter_context(tc.tile_pool(name="keep", bufs=1))
+        small = ctx.enter_context(tc.tile_pool(name="small", bufs=2))
+        w_pool = ctx.enter_context(tc.tile_pool(name="w_pool", bufs=W_BUFS))
+        wg_pool = ctx.enter_context(tc.tile_pool(name="wg_pool", bufs=3))
+        z_pool = ctx.enter_context(tc.tile_pool(name="z_pool", bufs=8))
+        planes_pool = ctx.enter_context(tc.tile_pool(name="planes_pool", bufs=2))
+        xg_pool = ctx.enter_context(tc.tile_pool(name="xg_pool", bufs=3))
+        y_pool = ctx.enter_context(tc.tile_pool(name="y_pool", bufs=4))
+        wt_psum = ctx.enter_context(tc.psum_pool(name="wt_psum", bufs=4))
+        work_psum = ctx.enter_context(tc.psum_pool(name="work_psum", bufs=4))
+        ctx.enter_context(tc.manual_schedule())
+
+        gb_raw = const.tile([P, 256], BF16)
+        nc.vector.memset(gb_raw[:], 0.0)
+        eps = const.tile([P, 1], F32)
+        nc.vector.memset(eps[:], EPS)
+        nc.sync.dma_start(out=gb_raw[0:16, :], in_=gamma.rearrange("(c k) -> c k", k=256))
+        nc.sync.dma_start(out=gb_raw[16:32, :], in_=beta.rearrange("(c k) -> c k", k=256))
+        gain_bf = [const.tile([P, 1], BF16, name="gain_bf%d" % part) for part in range(2)]
+        nc.scalar.dma_start(out=gain_bf[REAL][:], in_=s_re.partition_broadcast(P))
+        nc.scalar.dma_start(out=gain_bf[IMAG][:], in_=s_im.partition_broadcast(P))
+        warm = const.tile([P, 1], F32)
+        nc.scalar.activation(out=warm[:], in_=eps[:], func=ACT.Sqrt)
+
+        ident = const.tile([P, P], F32)
+        make_identity(nc, ident[:])
+
+        x_raw = [keep.tile([P, 2, D], BF16, name="x_raw%d" % tok) for tok in range(TOKEN_TILES)]
+
+        def load_x(tok):
+            for h in range(2):
+                nc.sync.dma_start(out=x_raw[tok][:, h, :], in_=x_streams[h][tok * P : (tok + 1) * P, :])
+
+        w_raw = {}
+
+        def load_chunk(c):
+            rnd, matrix = divmod(c, 2)
+            raw = w_pool.tile([P, 2, D], BF16)
+            rows = weights[matrix][rnd * N_CHUNK : (rnd + 1) * N_CHUNK, :]
+            nc.sync.dma_start(out=raw[:], in_=rows.rearrange("(r p) k -> p r k", p=P))
+            w_raw[c] = raw
+
+        load_x(0)
+        for c in range(4):
+            load_chunk(c)
+        load_x(1)
+        load_chunk(4)
+
+        gb_f32 = const.tile([P, 2, P], F32)
+        nc.gpsimd.tensor_copy(out=gb_f32[:], in_=gb_raw[:].rearrange("p (j e) -> p e j", e=2))
+        gb_ps = work_psum.tile([P, 2, P], F32, tag="work")
+        for e in range(2):
+            nc.tensor.transpose(gb_ps[:, e, :], gb_f32[:, e, :], ident[:])
+        gb_t = const.tile([P, 2, 32], F32)
+        nc.scalar.copy(out=gb_t[:], in_=gb_ps[:, :, 0:32])
+        gain = [const.tile([P, 1], F32, name="gain%d" % part) for part in range(2)]
+        for part in range(2):
+            nc.gpsimd.tensor_copy(out=gain[part][:], in_=gain_bf[part][:])
+
+        w_codes = [keep.tile([P, PASSES * N_CHUNK], U32, name="w_codes%d" % c, align_bytes=64) for c in range(CHUNKS)]
+        w_scales = [keep.tile([P, PASSES * N_CHUNK], U8, name="w_scales%d" % c, align_bytes=64) for c in range(CHUNKS)]
+        w_grouped = {}
+
+        def transpose_chunk(c):
+            words = w_raw[c][:].bitcast(F32)
+            grouped = wg_pool.tile([P, PASSES, N_CHUNK, 4], BF16, align_bytes=64)
+            grouped_words = grouped[:].bitcast(F32)
+            for g in range(PASSES):
+                bank = wt_psum.tile([P, 2, N_CHUNK], F32)
+                for r in range(2):
+                    for u in range(2):
+                        first = 256 * g + 128 * u
+                        nc.tensor.transpose(
+                            bank[:, u, r * P : (r + 1) * P], words[:, r, first : first + P], ident[:]
+                        )
+                nc.scalar.copy(out=grouped_words[:, g, :, :], in_=bank[:].rearrange("p u n -> p n u"))
+            w_grouped[c] = grouped
+
+        def quantise_chunk(c):
+            nc.vector.quantize_mx(
+                out=w_codes[c][:].bitcast(FP8X4),
+                scales=w_scales[c][:],
+                in_=w_grouped[c][:].rearrange("p g n t -> p (g n t)"),
+            )
+
+        def advance_weights(c):
+            if c < CHUNKS:
+                transpose_chunk(c)
+                if c + W_BUFS < CHUNKS:
+                    load_chunk(c + W_BUFS)
+            if 1 <= c <= CHUNKS:
+                quantise_chunk(c - 1)
+
+        a_codes = [[keep.tile([P, PASSES * P], U32, name="a_codes%d_%d" % (tok, op), align_bytes=64) for op in range(3)] for tok in range(TOKEN_TILES)]
+        a_scales = [[keep.tile([P, PASSES * P], U8, name="a_scales%d_%d" % (tok, op), align_bytes=64) for op in range(3)] for tok in range(TOKEN_TILES)]
+        stats = {}
+        row = {}
+        z_tiles = {}
+        planes = {}
+        x_grouped = {}
+
+        def statistics_part(tok, first, count):
+            if first == 0:
+                st = small.tile([P, 8, 6], F32)
+                stats[tok] = st
+            for i in range(first, first + count):
+                h, j = divmod(i, 4)
+                nc.vector.bn_stats(out=stats[tok][:, i, :], in_=x_raw[tok][:, h, 512 * j : 512 * (j + 1)])
+
+        def statistics_end(tok):
+            mv = small.tile([P, 2], F32)
+            nc.vector.bn_aggr(out=mv[:], in_=stats[tok][:].rearrange("p c s -> p (c s)"))
+            std = small.tile([P, 1], F32)
+            nc.scalar.activation(out=std[:], in_=mv[:, 1:2], func=ACT.Sqrt, bias=eps[:, 0:1], scale=1.0)
+            rstd = small.tile([P, 1], F32)
+            nc.vector.reciprocal(out=rstd[:], in_=std[:])
+            shift = small.tile([P, 1], F32)
+            nc.vector.tensor_scalar(
+                out=shift[:], in0=mv[:, 0:1], scalar1=rstd[:, 0:1], scalar2=-1.0, op0=ALU.mult, op1=ALU.mult
+            )
+            row[tok] = (rstd, shift)
+
+        def centre(tok, piece):
+            h, g = divmod(piece, PASSES)
+            rstd, shift = row[tok]
+            z = z_pool.tile([P, 4, P], F32)
+            nc.gpsimd.tensor_scalar(
+                out=z[:].rearrange("p (u e) j -> p u e j", e=2),
+                in0=x_raw[tok][:, h, K_PASS * g : K_PASS * (g + 1)].rearrange("p (u j e) -> p u e j", u=2, e=2),
+                scalar1=rstd[:, 0:1],
+                scalar2=shift[:, 0:1],
+                op0=ALU.mult,
+                op1=ALU.add,
+            )
+            z_tiles[(tok, piece)] = z
+
+        def quantise_operand(tok, op, grouped):
+            nc.vector.quantize_mx(
+                out=a_codes[tok][op][:].bitcast(FP8X4),
+                scales=a_scales[tok][op][:],
+                in_=grouped[:].rearrange("p g k t -> p (g k t)"),
+            )
+
+        def normalise_piece(tok, piece):
+            h, g = divmod(piece, PASSES)
+            if g == 0:
+                pl = planes_pool.tile([P, PASSES, 4, P], BF16)
+                planes[(tok, h)] = pl
+            z = z_tiles[(tok, piece)]
+            z_t = work_psum.tile([P, 4, P], F32, tag="work")
+            for t in range(4):
+                nc.tensor.transpose(z_t[:, t, :], z[:, t, :], ident[:])
+            for t in range(4):
+                u, e = divmod(t, 2)
+                c = 8 * h + 2 * g + u
+                nc.vector.tensor_scalar(
+                    out=planes[(tok, h)][:, g, t, :],
+                    in0=z_t[:, t, :],
+                    scalar1=gb_t[:, e, c : c + 1],
+                    scalar2=gb_t[:, e, 16 + c : 17 + c],
+                    op0=ALU.mult,
+                    op1=ALU.add,
+                )
+            if g == PASSES - 1:
+                grouped = xg_pool.tile([P, PASSES, P, 4], BF16, align_bytes=64)
+                nc.vector.tensor_copy(out=grouped[:], in_=planes[(tok, h)][:].rearrange("p g t k -> p g k t"))
+                x_grouped[(tok, h)] = grouped
+                if h == 1:
+                    quantise_operand(tok, NR, x_grouped[(tok, 0)])
+                    negated = xg_pool.tile([P, PASSES, P, 4], BF16, align_bytes=64, tag="grouped")
+                    nc.vector.tensor_scalar(
+                        out=negated[:].rearrange("p g k t -> p (g k t)"),
+                        in0=grouped[:].rearrange("p g k t -> p (g k t)"),
+                        scalar1=-1.0,
+                        scalar2=None,
+                        op0=ALU.mult,
+                    )
+                    quantise_operand(tok, NI, grouped)
+                    quantise_operand(tok, NEG_NI, negated)
+
+        acc = {}
+
+        def multiply(tok, step):
+            rnd = step // 2
+            part = (IMAG, REAL)[step % 2]
+            if rnd % 2 == 0:
+                bank = work_psum.tile([P, ACC_COLS], F32, tag="work")
+                acc[part] = bank
+            half = rnd % 2
+            cols = acc[part][:, half * N_CHUNK : (half + 1) * N_CHUNK]
+            pairs = ((NR, REAL), (NEG_NI, IMAG)) if part == REAL else ((NR, IMAG), (NI, REAL))
+            for i, (op, matrix) in enumerate(pairs):
+                c = 2 * rnd + matrix
+                for g in range(PASSES):
+                    nc.tensor.matmul_mx(
+                        out=cols,
+                        lhsT=a_codes[tok][op][:, g * P : (g + 1) * P].bitcast(FP8X4),
+                        lhsT_scale=a_scales[tok][op][:, g * P : (g + 1) * P],
+                        rhs=w_codes[c][:, g * N_CHUNK : (g + 1) * N_CHUNK].bitcast(FP8X4),
+                        rhs_scale=w_scales[c][:, g * N_CHUNK : (g + 1) * N_CHUNK],
+                        start=(i == 0 and g == 0),
+                        stop=(i == 1 and g == PASSES - 1),
+                    )
+            if half == 1:
+                y = y_pool.tile([P, ACC_COLS], F32)
+                nc.scalar.activation(out=y[:], in_=acc[part][:], func=ACT.Copy, scale=gain[part][:, 0:1])
+                first = (rnd // 2) * ACC_COLS
+                nc.scalar.dma_start(out=outs[part][tok * P : (tok + 1) * P, first : first + ACC_COLS], in_=y[:])
+
+        statistics_part(0, 0, 8)
+        statistics_end(0)
+        for piece in range(8):
+            centre(0, piece)
+        advance_weights(0)
+        advance_weights(1)
+        for piece in range(4):
+            normalise_piece(0, piece)
+        advance_weights(2)
+        for piece in range(4, 8):
+            normalise_piece(0, piece)
+        advance_weights(3)
+
+        for step in range(2 * ROUNDS):
+            advance_weights(LEAD + step)
+            if step < 4:
+                statistics_part(1, 2 * step, 2)
+            if step == 3:
+                statistics_end(1)
+                for piece in range(8):
+                    centre(1, piece)
+            if 4 <= step < 12:
+                normalise_piece(1, step - 4)
+            multiply(0, step)
+        for step in range(2 * ROUNDS):
+            multiply(1, step)

@@ -18,15 +18,23 @@ D = 2048
 N_OUT = 2048
 EPS = 1e-6
 
-K_PASS = 512
+PACK = 4
+K_PASS = P * PACK
 PASSES = D // K_PASS
+PIECES = 2 * PASSES
 N_CHUNK = 256
 ROUNDS = N_OUT // N_CHUNK
 CHUNKS = 2 * ROUNDS
+STEPS = 2 * ROUNDS
 ACC_COLS = 512
+BN_COLS = 512
 
 W_BUFS = 5
-LEAD = 4
+T_LEAD = 4
+Q_LEAD = 3
+X1_AFTER_CHUNK = 5
+STATS_STEPS = 2
+PIECE_STEP = 5
 
 NR, NI, NEG_NI = 0, 1, 2
 REAL, IMAG = 0, 1
@@ -48,7 +56,7 @@ def tile_realimagfourvallinear_pa_kernel(
         small = ctx.enter_context(tc.tile_pool(name="small", bufs=2))
         w_pool = ctx.enter_context(tc.tile_pool(name="w_pool", bufs=W_BUFS))
         wg_pool = ctx.enter_context(tc.tile_pool(name="wg_pool", bufs=3))
-        z_pool = ctx.enter_context(tc.tile_pool(name="z_pool", bufs=8))
+        z_pool = ctx.enter_context(tc.tile_pool(name="z_pool", bufs=PIECES))
         planes_pool = ctx.enter_context(tc.tile_pool(name="planes_pool", bufs=2))
         xg_pool = ctx.enter_context(tc.tile_pool(name="xg_pool", bufs=3))
         y_pool = ctx.enter_context(tc.tile_pool(name="y_pool", bufs=4))
@@ -58,18 +66,11 @@ def tile_realimagfourvallinear_pa_kernel(
 
         gb_raw = const.tile([P, 256], BF16)
         nc.vector.memset(gb_raw[:], 0.0)
-        eps = const.tile([P, 1], F32)
-        nc.vector.memset(eps[:], EPS)
         nc.sync.dma_start(out=gb_raw[0:16, :], in_=gamma.rearrange("(c k) -> c k", k=256))
         nc.sync.dma_start(out=gb_raw[16:32, :], in_=beta.rearrange("(c k) -> c k", k=256))
         gain_bf = [const.tile([P, 1], BF16, name="gain_bf%d" % part) for part in range(2)]
         nc.scalar.dma_start(out=gain_bf[REAL][:], in_=s_re.partition_broadcast(P))
         nc.scalar.dma_start(out=gain_bf[IMAG][:], in_=s_im.partition_broadcast(P))
-        warm = const.tile([P, 1], F32)
-        nc.scalar.activation(out=warm[:], in_=eps[:], func=ACT.Sqrt)
-
-        ident = const.tile([P, P], F32)
-        make_identity(nc, ident[:])
 
         x_raw = [keep.tile([P, 2, D], BF16, name="x_raw%d" % tok) for tok in range(TOKEN_TILES)]
 
@@ -85,13 +86,17 @@ def tile_realimagfourvallinear_pa_kernel(
             rows = weights[matrix][rnd * N_CHUNK : (rnd + 1) * N_CHUNK, :]
             nc.sync.dma_start(out=raw[:], in_=rows.rearrange("(r p) k -> p r k", p=P))
             w_raw[c] = raw
+            if c == X1_AFTER_CHUNK:
+                load_x(1)
 
         load_x(0)
-        for c in range(4):
+        for c in range(W_BUFS):
             load_chunk(c)
-        load_x(1)
-        load_chunk(4)
 
+        ident = const.tile([P, P], F32)
+        make_identity(nc, ident[:])
+        minus_half = const.tile([P, 1], F32)
+        nc.gpsimd.memset(minus_half[:], -0.5)
         gb_f32 = const.tile([P, 2, P], F32)
         nc.gpsimd.tensor_copy(out=gb_f32[:], in_=gb_raw[:].rearrange("p (j e) -> p e j", e=2))
         gb_ps = work_psum.tile([P, 2, P], F32, tag="work")
@@ -103,24 +108,30 @@ def tile_realimagfourvallinear_pa_kernel(
         for part in range(2):
             nc.gpsimd.tensor_copy(out=gain[part][:], in_=gain_bf[part][:])
 
-        w_codes = [keep.tile([P, PASSES * N_CHUNK], U32, name="w_codes%d" % c, align_bytes=64) for c in range(CHUNKS)]
-        w_scales = [keep.tile([P, PASSES * N_CHUNK], U8, name="w_scales%d" % c, align_bytes=64) for c in range(CHUNKS)]
+        w_codes = [
+            keep.tile([P, PASSES * N_CHUNK], U32, name="w_codes%d" % c, align_bytes=64) for c in range(CHUNKS)
+        ]
+        w_scales = [
+            keep.tile([P, PASSES * N_CHUNK], U8, name="w_scales%d" % c, align_bytes=64) for c in range(CHUNKS)
+        ]
         w_grouped = {}
 
         def transpose_chunk(c):
             words = w_raw[c][:].bitcast(F32)
-            grouped = wg_pool.tile([P, PASSES, N_CHUNK, 4], BF16, align_bytes=64)
+            grouped = wg_pool.tile([P, PASSES, N_CHUNK, PACK], BF16, align_bytes=64)
             grouped_words = grouped[:].bitcast(F32)
             for g in range(PASSES):
                 bank = wt_psum.tile([P, 2, N_CHUNK], F32)
                 for r in range(2):
                     for u in range(2):
-                        first = 256 * g + 128 * u
+                        first = 256 * g + P * u
                         nc.tensor.transpose(
                             bank[:, u, r * P : (r + 1) * P], words[:, r, first : first + P], ident[:]
                         )
                 nc.scalar.copy(out=grouped_words[:, g, :, :], in_=bank[:].rearrange("p u n -> p n u"))
             w_grouped[c] = grouped
+            if c + W_BUFS < CHUNKS:
+                load_chunk(c + W_BUFS)
 
         def quantise_chunk(c):
             nc.vector.quantize_mx(
@@ -129,56 +140,47 @@ def tile_realimagfourvallinear_pa_kernel(
                 in_=w_grouped[c][:].rearrange("p g n t -> p (g n t)"),
             )
 
-        def advance_weights(c):
-            if c < CHUNKS:
-                transpose_chunk(c)
-                if c + W_BUFS < CHUNKS:
-                    load_chunk(c + W_BUFS)
-            if 1 <= c <= CHUNKS:
-                quantise_chunk(c - 1)
-
-        a_codes = [[keep.tile([P, PASSES * P], U32, name="a_codes%d_%d" % (tok, op), align_bytes=64) for op in range(3)] for tok in range(TOKEN_TILES)]
-        a_scales = [[keep.tile([P, PASSES * P], U8, name="a_scales%d_%d" % (tok, op), align_bytes=64) for op in range(3)] for tok in range(TOKEN_TILES)]
-        stats = {}
-        row = {}
+        a_codes = [
+            [keep.tile([P, PASSES * P], U32, name="a_codes%d_%d" % (tok, op), align_bytes=64) for op in range(3)]
+            for tok in range(TOKEN_TILES)
+        ]
+        a_scales = [
+            [keep.tile([P, PASSES * P], U8, name="a_scales%d_%d" % (tok, op), align_bytes=64) for op in range(3)]
+            for tok in range(TOKEN_TILES)
+        ]
+        stats = [keep.tile([P, 2 * D // BN_COLS, 6], F32, name="stats%d" % tok) for tok in range(TOKEN_TILES)]
         z_tiles = {}
         planes = {}
         x_grouped = {}
 
-        def statistics_part(tok, first, count):
-            if first == 0:
-                st = small.tile([P, 8, 6], F32)
-                stats[tok] = st
-            for i in range(first, first + count):
-                h, j = divmod(i, 4)
-                nc.vector.bn_stats(out=stats[tok][:, i, :], in_=x_raw[tok][:, h, 512 * j : 512 * (j + 1)])
+        def statistics(tok, parts):
+            for i in parts:
+                h, j = divmod(i, D // BN_COLS)
+                nc.vector.bn_stats(out=stats[tok][:, i, :], in_=x_raw[tok][:, h, BN_COLS * j : BN_COLS * (j + 1)])
 
-        def statistics_end(tok):
+        def centre(tok):
             mv = small.tile([P, 2], F32)
             nc.vector.bn_aggr(out=mv[:], in_=stats[tok][:].rearrange("p c s -> p (c s)"))
-            std = small.tile([P, 1], F32)
-            nc.scalar.activation(out=std[:], in_=mv[:, 1:2], func=ACT.Sqrt, bias=eps[:, 0:1], scale=1.0)
+            var_eps = small.tile([P, 1], F32)
+            nc.gpsimd.tensor_scalar(out=var_eps[:], in0=mv[:, 1:2], scalar1=EPS, scalar2=None, op0=ALU.add)
             rstd = small.tile([P, 1], F32)
-            nc.vector.reciprocal(out=rstd[:], in_=std[:])
+            nc.gpsimd.tensor_tensor(out=rstd[:], in0=var_eps[:], in1=minus_half[:], op=ALU.pow)
             shift = small.tile([P, 1], F32)
-            nc.vector.tensor_scalar(
+            nc.gpsimd.tensor_scalar(
                 out=shift[:], in0=mv[:, 0:1], scalar1=rstd[:, 0:1], scalar2=-1.0, op0=ALU.mult, op1=ALU.mult
             )
-            row[tok] = (rstd, shift)
-
-        def centre(tok, piece):
-            h, g = divmod(piece, PASSES)
-            rstd, shift = row[tok]
-            z = z_pool.tile([P, 4, P], F32)
-            nc.gpsimd.tensor_scalar(
-                out=z[:].rearrange("p (u e) j -> p u e j", e=2),
-                in0=x_raw[tok][:, h, K_PASS * g : K_PASS * (g + 1)].rearrange("p (u j e) -> p u e j", u=2, e=2),
-                scalar1=rstd[:, 0:1],
-                scalar2=shift[:, 0:1],
-                op0=ALU.mult,
-                op1=ALU.add,
-            )
-            z_tiles[(tok, piece)] = z
+            for piece in range(PIECES):
+                h, g = divmod(piece, PASSES)
+                z = z_pool.tile([P, PACK, P], F32)
+                nc.gpsimd.tensor_scalar(
+                    out=z[:].rearrange("p (u e) j -> p u e j", e=2),
+                    in0=x_raw[tok][:, h, K_PASS * g : K_PASS * (g + 1)].rearrange("p (u j e) -> p u e j", u=2, e=2),
+                    scalar1=rstd[:, 0:1],
+                    scalar2=shift[:, 0:1],
+                    op0=ALU.mult,
+                    op1=ALU.add,
+                )
+                z_tiles[(tok, piece)] = z
 
         def quantise_operand(tok, op, grouped):
             nc.vector.quantize_mx(
@@ -190,49 +192,58 @@ def tile_realimagfourvallinear_pa_kernel(
         def normalise_piece(tok, piece):
             h, g = divmod(piece, PASSES)
             if g == 0:
-                pl = planes_pool.tile([P, PASSES, 4, P], BF16)
-                planes[(tok, h)] = pl
+                stream_planes = planes_pool.tile([P, PASSES, PACK, P], BF16)
+                planes[(tok, h)] = stream_planes
             z = z_tiles[(tok, piece)]
-            z_t = work_psum.tile([P, 4, P], F32, tag="work")
-            for t in range(4):
+            z_t = work_psum.tile([P, PACK, P], F32, tag="work")
+            for t in range(PACK):
                 nc.tensor.transpose(z_t[:, t, :], z[:, t, :], ident[:])
-            for t in range(4):
+            for t in range(PACK):
                 u, e = divmod(t, 2)
-                c = 8 * h + 2 * g + u
-                nc.vector.tensor_scalar(
-                    out=planes[(tok, h)][:, g, t, :],
-                    in0=z_t[:, t, :],
-                    scalar1=gb_t[:, e, c : c + 1],
-                    scalar2=gb_t[:, e, 16 + c : 17 + c],
-                    op0=ALU.mult,
-                    op1=ALU.add,
-                )
+                c = PIECES * h + 2 * g + u
+                if tok == 0 and piece % 2 == 1:
+                    nc.scalar.activation(
+                        out=planes[(tok, h)][:, g, t, :],
+                        in_=z_t[:, t, :],
+                        func=ACT.Identity,
+                        scale=gb_t[:, e, c : c + 1],
+                        bias=gb_t[:, e, 16 + c : 17 + c],
+                    )
+                else:
+                    nc.vector.tensor_scalar(
+                        out=planes[(tok, h)][:, g, t, :],
+                        in0=z_t[:, t, :],
+                        scalar1=gb_t[:, e, c : c + 1],
+                        scalar2=gb_t[:, e, 16 + c : 17 + c],
+                        op0=ALU.mult,
+                        op1=ALU.add,
+                    )
             if g == PASSES - 1:
-                grouped = xg_pool.tile([P, PASSES, P, 4], BF16, align_bytes=64)
+                grouped = xg_pool.tile([P, PASSES, P, PACK], BF16, align_bytes=64)
                 nc.vector.tensor_copy(out=grouped[:], in_=planes[(tok, h)][:].rearrange("p g t k -> p g k t"))
                 x_grouped[(tok, h)] = grouped
-                if h == 1:
-                    quantise_operand(tok, NR, x_grouped[(tok, 0)])
-                    negated = xg_pool.tile([P, PASSES, P, 4], BF16, align_bytes=64, tag="grouped")
-                    nc.vector.tensor_scalar(
-                        out=negated[:].rearrange("p g k t -> p (g k t)"),
-                        in0=grouped[:].rearrange("p g k t -> p (g k t)"),
-                        scalar1=-1.0,
-                        scalar2=None,
-                        op0=ALU.mult,
-                    )
-                    quantise_operand(tok, NI, grouped)
-                    quantise_operand(tok, NEG_NI, negated)
+            if piece == PIECES - 1:
+                quantise_operand(tok, NR, x_grouped[(tok, REAL)])
+                quantise_operand(tok, NI, x_grouped[(tok, IMAG)])
+                negated = xg_pool.tile([P, PASSES, P, PACK], BF16, align_bytes=64, tag="grouped")
+                nc.vector.tensor_scalar(
+                    out=negated[:].rearrange("p g k t -> p (g k t)"),
+                    in0=x_grouped[(tok, IMAG)][:].rearrange("p g k t -> p (g k t)"),
+                    scalar1=-1.0,
+                    scalar2=None,
+                    op0=ALU.mult,
+                )
+                quantise_operand(tok, NEG_NI, negated)
 
         acc = {}
 
         def multiply(tok, step):
             rnd = step // 2
             part = (IMAG, REAL)[step % 2]
-            if rnd % 2 == 0:
+            half = rnd % 2
+            if half == 0:
                 bank = work_psum.tile([P, ACC_COLS], F32, tag="work")
                 acc[part] = bank
-            half = rnd % 2
             cols = acc[part][:, half * N_CHUNK : (half + 1) * N_CHUNK]
             pairs = ((NR, REAL), (NEG_NI, IMAG)) if part == REAL else ((NR, IMAG), (NI, REAL))
             for i, (op, matrix) in enumerate(pairs):
@@ -253,29 +264,33 @@ def tile_realimagfourvallinear_pa_kernel(
                 first = (rnd // 2) * ACC_COLS
                 nc.scalar.dma_start(out=outs[part][tok * P : (tok + 1) * P, first : first + ACC_COLS], in_=y[:])
 
-        statistics_part(0, 0, 8)
-        statistics_end(0)
-        for piece in range(8):
-            centre(0, piece)
-        advance_weights(0)
-        advance_weights(1)
-        for piece in range(4):
+        statistics(0, range(8))
+        centre(0)
+        transpose_chunk(0)
+        transpose_chunk(1)
+        quantise_chunk(0)
+        for piece in range(PASSES):
             normalise_piece(0, piece)
-        advance_weights(2)
-        for piece in range(4, 8):
+        transpose_chunk(2)
+        quantise_chunk(1)
+        for piece in range(PASSES, PIECES):
             normalise_piece(0, piece)
-        advance_weights(3)
+        transpose_chunk(3)
+        quantise_chunk(2)
 
-        for step in range(2 * ROUNDS):
-            advance_weights(LEAD + step)
-            if step < 4:
-                statistics_part(1, 2 * step, 2)
-            if step == 3:
-                statistics_end(1)
-                for piece in range(8):
-                    centre(1, piece)
-            if 4 <= step < 12:
-                normalise_piece(1, step - 4)
+        for step in range(STEPS):
+            if T_LEAD + step < CHUNKS:
+                transpose_chunk(T_LEAD + step)
+            if Q_LEAD + step < CHUNKS:
+                quantise_chunk(Q_LEAD + step)
+            if step < STATS_STEPS:
+                share = 8 // STATS_STEPS
+                statistics(1, range(share * step, share * (step + 1)))
+            if step == STATS_STEPS - 1:
+                centre(1)
+            if PIECE_STEP <= step < PIECE_STEP + PIECES:
+                normalise_piece(1, step - PIECE_STEP)
             multiply(0, step)
-        for step in range(2 * ROUNDS):
+
+        for step in range(STEPS):
             multiply(1, step)

@@ -29,6 +29,7 @@ STEPS = 2 * ROUNDS
 ACC_COLS = 512
 BN_COLS = 512
 
+WARM_UP = 4
 W_BUFS = 5
 T_LEAD = 4
 Q_LEAD = 3
@@ -108,6 +109,16 @@ def tile_realimagfourvallinear_pa_kernel(
         for part in range(2):
             nc.gpsimd.tensor_copy(out=gain[part][:], in_=gain_bf[part][:])
 
+        idle_in = const.tile([P, 512], BF16)
+        nc.vector.memset(idle_in[:], 0.0)
+        idle_out = work_psum.tile([P, 512], F32, tag="work")
+
+        def keep_clock_up(count=1):
+            for i in range(count):
+                nc.tensor.matmul(out=idle_out[:], lhsT=idle_in[:, 0:P], rhs=idle_in[:], start=True, stop=True)
+
+        keep_clock_up(WARM_UP)
+
         w_codes = [
             keep.tile([P, PASSES * N_CHUNK], U32, name="w_codes%d" % c, align_bytes=64) for c in range(CHUNKS)
         ]
@@ -129,6 +140,8 @@ def tile_realimagfourvallinear_pa_kernel(
                             bank[:, u, r * P : (r + 1) * P], words[:, r, first : first + P], ident[:]
                         )
                 nc.scalar.copy(out=grouped_words[:, g, :, :], in_=bank[:].rearrange("p u n -> p n u"))
+                if c < T_LEAD:
+                    keep_clock_up()
             w_grouped[c] = grouped
             if c + W_BUFS < CHUNKS:
                 load_chunk(c + W_BUFS)
@@ -198,6 +211,8 @@ def tile_realimagfourvallinear_pa_kernel(
             z_t = work_psum.tile([P, PACK, P], F32, tag="work")
             for t in range(PACK):
                 nc.tensor.transpose(z_t[:, t, :], z[:, t, :], ident[:])
+            if tok == 0:
+                keep_clock_up()
             for t in range(PACK):
                 u, e = divmod(t, 2)
                 c = PIECES * h + 2 * g + u
@@ -237,16 +252,17 @@ def tile_realimagfourvallinear_pa_kernel(
 
         acc = {}
 
-        def multiply(tok, step):
+        def multiply(tok, step, products=(0, 1)):
             rnd = step // 2
             part = (IMAG, REAL)[step % 2]
             half = rnd % 2
-            if half == 0:
+            if half == 0 and 0 in products:
                 bank = work_psum.tile([P, ACC_COLS], F32, tag="work")
                 acc[part] = bank
             cols = acc[part][:, half * N_CHUNK : (half + 1) * N_CHUNK]
             pairs = ((NR, REAL), (NEG_NI, IMAG)) if part == REAL else ((NR, IMAG), (NI, REAL))
-            for i, (op, matrix) in enumerate(pairs):
+            for i in products:
+                op, matrix = pairs[i]
                 c = 2 * rnd + matrix
                 for g in range(PASSES):
                     nc.tensor.matmul_mx(
@@ -258,7 +274,7 @@ def tile_realimagfourvallinear_pa_kernel(
                         start=(i == 0 and g == 0),
                         stop=(i == 1 and g == PASSES - 1),
                     )
-            if half == 1:
+            if half == 1 and 1 in products:
                 y = y_pool.tile([P, ACC_COLS], F32)
                 nc.scalar.activation(out=y[:], in_=acc[part][:], func=ACT.Copy, scale=gain[part][:, 0:1])
                 first = (rnd // 2) * ACC_COLS
@@ -288,9 +304,10 @@ def tile_realimagfourvallinear_pa_kernel(
                 statistics(1, range(share * step, share * (step + 1)))
             if step == STATS_STEPS - 1:
                 centre(1)
+            multiply(0, step, products=(0,))
             if PIECE_STEP <= step < PIECE_STEP + PIECES:
                 normalise_piece(1, step - PIECE_STEP)
-            multiply(0, step)
+            multiply(0, step, products=(1,))
 
         for step in range(STEPS):
             multiply(1, step)

@@ -29,7 +29,6 @@ STEPS = 2 * ROUNDS
 ACC_COLS = 512
 BN_COLS = 512
 
-WARM_UP = 4
 W_BUFS = 5
 T_LEAD = 4
 Q_LEAD = 3
@@ -109,16 +108,6 @@ def tile_realimagfourvallinear_pa_kernel(
         for part in range(2):
             nc.gpsimd.tensor_copy(out=gain[part][:], in_=gain_bf[part][:])
 
-        idle_in = const.tile([P, 512], BF16)
-        nc.vector.memset(idle_in[:], 0.0)
-        idle_out = work_psum.tile([P, 512], F32, tag="work")
-
-        def keep_clock_up(count=1):
-            for i in range(count):
-                nc.tensor.matmul(out=idle_out[:], lhsT=idle_in[:, 0:P], rhs=idle_in[:], start=True, stop=True)
-
-        keep_clock_up(WARM_UP)
-
         w_codes = [
             keep.tile([P, PASSES * N_CHUNK], U32, name="w_codes%d" % c, align_bytes=64) for c in range(CHUNKS)
         ]
@@ -140,8 +129,6 @@ def tile_realimagfourvallinear_pa_kernel(
                             bank[:, u, r * P : (r + 1) * P], words[:, r, first : first + P], ident[:]
                         )
                 nc.scalar.copy(out=grouped_words[:, g, :, :], in_=bank[:].rearrange("p u n -> p n u"))
-                if c < T_LEAD:
-                    keep_clock_up()
             w_grouped[c] = grouped
             if c + W_BUFS < CHUNKS:
                 load_chunk(c + W_BUFS)
@@ -175,23 +162,22 @@ def tile_realimagfourvallinear_pa_kernel(
             mv = small.tile([P, 2], F32)
             nc.vector.bn_aggr(out=mv[:], in_=stats[tok][:].rearrange("p c s -> p (c s)"))
             var_eps = small.tile([P, 1], F32)
-            nc.gpsimd.tensor_scalar(out=var_eps[:], in0=mv[:, 1:2], scalar1=EPS, scalar2=None, op0=ALU.add)
+            nc.vector.tensor_scalar(out=var_eps[:], in0=mv[:, 1:2], scalar1=EPS, scalar2=None, op0=ALU.add)
+            minus_mean = small.tile([P, 1], F32)
+            nc.vector.tensor_scalar(out=minus_mean[:], in0=mv[:, 0:1], scalar1=-1.0, scalar2=None, op0=ALU.mult)
             rstd = small.tile([P, 1], F32)
             nc.gpsimd.tensor_tensor(out=rstd[:], in0=var_eps[:], in1=minus_half[:], op=ALU.pow)
-            shift = small.tile([P, 1], F32)
-            nc.gpsimd.tensor_scalar(
-                out=shift[:], in0=mv[:, 0:1], scalar1=rstd[:, 0:1], scalar2=-1.0, op0=ALU.mult, op1=ALU.mult
-            )
             for piece in range(PIECES):
                 h, g = divmod(piece, PASSES)
                 z = z_pool.tile([P, PACK, P], F32)
-                nc.gpsimd.tensor_scalar(
+                engine = nc.vector if tok == 0 and h == REAL else nc.gpsimd
+                engine.tensor_scalar(
                     out=z[:].rearrange("p (u e) j -> p u e j", e=2),
                     in0=x_raw[tok][:, h, K_PASS * g : K_PASS * (g + 1)].rearrange("p (u j e) -> p u e j", u=2, e=2),
-                    scalar1=rstd[:, 0:1],
-                    scalar2=shift[:, 0:1],
-                    op0=ALU.mult,
-                    op1=ALU.add,
+                    scalar1=minus_mean[:, 0:1],
+                    scalar2=rstd[:, 0:1],
+                    op0=ALU.add,
+                    op1=ALU.mult,
                 )
                 z_tiles[(tok, piece)] = z
 
@@ -211,8 +197,6 @@ def tile_realimagfourvallinear_pa_kernel(
             z_t = work_psum.tile([P, PACK, P], F32, tag="work")
             for t in range(PACK):
                 nc.tensor.transpose(z_t[:, t, :], z[:, t, :], ident[:])
-            if tok == 0:
-                keep_clock_up()
             for t in range(PACK):
                 u, e = divmod(t, 2)
                 c = PIECES * h + 2 * g + u
@@ -252,17 +236,16 @@ def tile_realimagfourvallinear_pa_kernel(
 
         acc = {}
 
-        def multiply(tok, step, products=(0, 1)):
+        def multiply(tok, step):
             rnd = step // 2
             part = (IMAG, REAL)[step % 2]
             half = rnd % 2
-            if half == 0 and 0 in products:
+            if half == 0:
                 bank = work_psum.tile([P, ACC_COLS], F32, tag="work")
                 acc[part] = bank
             cols = acc[part][:, half * N_CHUNK : (half + 1) * N_CHUNK]
             pairs = ((NR, REAL), (NEG_NI, IMAG)) if part == REAL else ((NR, IMAG), (NI, REAL))
-            for i in products:
-                op, matrix = pairs[i]
+            for i, (op, matrix) in enumerate(pairs):
                 c = 2 * rnd + matrix
                 for g in range(PASSES):
                     nc.tensor.matmul_mx(
@@ -274,7 +257,7 @@ def tile_realimagfourvallinear_pa_kernel(
                         start=(i == 0 and g == 0),
                         stop=(i == 1 and g == PASSES - 1),
                     )
-            if half == 1 and 1 in products:
+            if half == 1:
                 y = y_pool.tile([P, ACC_COLS], F32)
                 nc.scalar.activation(out=y[:], in_=acc[part][:], func=ACT.Copy, scale=gain[part][:, 0:1])
                 first = (rnd // 2) * ACC_COLS
@@ -304,10 +287,9 @@ def tile_realimagfourvallinear_pa_kernel(
                 statistics(1, range(share * step, share * (step + 1)))
             if step == STATS_STEPS - 1:
                 centre(1)
-            multiply(0, step, products=(0,))
             if PIECE_STEP <= step < PIECE_STEP + PIECES:
                 normalise_piece(1, step - PIECE_STEP)
-            multiply(0, step, products=(1,))
+            multiply(0, step)
 
         for step in range(STEPS):
             multiply(1, step)

@@ -261,7 +261,7 @@ def tile_realimagfourvallinear_pa_kernel(
                 y = y_pool.tile([P, ACC_COLS], F32)
                 nc.scalar.activation(out=y[:], in_=acc[part][:], func=ACT.Copy, scale=gain[part][:, 0:1])
                 first = (rnd // 2) * ACC_COLS
-                nc.scalar.dma_start(out=outs[part][tok * P : (tok + 1) * P, first : first + ACC_COLS], in_=y[:])
+                nc.sync.dma_start(out=outs[part][tok * P : (tok + 1) * P, first : first + ACC_COLS], in_=y[:])
 
         statistics(0, range(8))
         centre(0)

@@ -18,6 +18,9 @@ D = 2048
 N_OUT = 2048
 EPS = 1e-6
 
+REAL, IMAG = 0, 1
+NR, NI, NEG_NI = 0, 1, 2
+
 PACK = 4
 K_PASS = P * PACK
 PASSES = D // K_PASS
@@ -26,18 +29,18 @@ N_CHUNK = 256
 ROUNDS = N_OUT // N_CHUNK
 CHUNKS = 2 * ROUNDS
 STEPS = 2 * ROUNDS
-ACC_COLS = 512
+ACC_COLS = 2 * N_CHUNK
 BN_COLS = 512
+BN_PARTS = 2 * D // BN_COLS
+GB_COLS = 2 * P
+GB_ROWS = 2 * D // GB_COLS
 
 W_BUFS = 5
 T_LEAD = 4
-Q_LEAD = 3
+Q_LEAD = T_LEAD - 1
 X1_AFTER_CHUNK = 5
-STATS_STEPS = 2
-PIECE_STEP = 5
-
-NR, NI, NEG_NI = 0, 1, 2
-REAL, IMAG = 0, 1
+STATS_STEPS = 4
+PIECE_STEP = STATS_STEPS + 1
 
 FLOPS = 4 * 2 * TOKENS * D * N_OUT
 
@@ -64,10 +67,10 @@ def tile_realimagfourvallinear_pa_kernel(
         work_psum = ctx.enter_context(tc.psum_pool(name="work_psum", bufs=4))
         ctx.enter_context(tc.manual_schedule())
 
-        gb_raw = const.tile([P, 256], BF16)
+        gb_raw = const.tile([P, GB_COLS], BF16)
         nc.vector.memset(gb_raw[:], 0.0)
-        nc.sync.dma_start(out=gb_raw[0:16, :], in_=gamma.rearrange("(c k) -> c k", k=256))
-        nc.sync.dma_start(out=gb_raw[16:32, :], in_=beta.rearrange("(c k) -> c k", k=256))
+        nc.sync.dma_start(out=gb_raw[0:GB_ROWS, :], in_=gamma.rearrange("(c k) -> c k", k=GB_COLS))
+        nc.sync.dma_start(out=gb_raw[GB_ROWS : 2 * GB_ROWS, :], in_=beta.rearrange("(c k) -> c k", k=GB_COLS))
         gain_bf = [const.tile([P, 1], BF16, name="gain_bf%d" % part) for part in range(2)]
         nc.scalar.dma_start(out=gain_bf[REAL][:], in_=s_re.partition_broadcast(P))
         nc.scalar.dma_start(out=gain_bf[IMAG][:], in_=s_im.partition_broadcast(P))
@@ -75,8 +78,10 @@ def tile_realimagfourvallinear_pa_kernel(
         x_raw = [keep.tile([P, 2, D], BF16, name="x_raw%d" % tok) for tok in range(TOKEN_TILES)]
 
         def load_x(tok):
-            for h in range(2):
-                nc.sync.dma_start(out=x_raw[tok][:, h, :], in_=x_streams[h][tok * P : (tok + 1) * P, :])
+            for stream in range(2):
+                nc.sync.dma_start(
+                    out=x_raw[tok][:, stream, :], in_=x_streams[stream][tok * P : (tok + 1) * P, :]
+                )
 
         w_raw = {}
 
@@ -102,8 +107,8 @@ def tile_realimagfourvallinear_pa_kernel(
         gb_ps = work_psum.tile([P, 2, P], F32, tag="work")
         for e in range(2):
             nc.tensor.transpose(gb_ps[:, e, :], gb_f32[:, e, :], ident[:])
-        gb_t = const.tile([P, 2, 32], F32)
-        nc.scalar.copy(out=gb_t[:], in_=gb_ps[:, :, 0:32])
+        gb_t = const.tile([P, 2, 2 * GB_ROWS], F32)
+        nc.scalar.copy(out=gb_t[:], in_=gb_ps[:, :, 0 : 2 * GB_ROWS])
         gain = [const.tile([P, 1], F32, name="gain%d" % part) for part in range(2)]
         for part in range(2):
             nc.gpsimd.tensor_copy(out=gain[part][:], in_=gain_bf[part][:])
@@ -124,9 +129,9 @@ def tile_realimagfourvallinear_pa_kernel(
                 bank = wt_psum.tile([P, 2, N_CHUNK], F32)
                 for r in range(2):
                     for u in range(2):
-                        first = 256 * g + P * u
+                        first_word = 2 * P * g + P * u
                         nc.tensor.transpose(
-                            bank[:, u, r * P : (r + 1) * P], words[:, r, first : first + P], ident[:]
+                            bank[:, u, r * P : (r + 1) * P], words[:, r, first_word : first_word + P], ident[:]
                         )
                 nc.scalar.copy(out=grouped_words[:, g, :, :], in_=bank[:].rearrange("p u n -> p n u"))
             w_grouped[c] = grouped
@@ -148,15 +153,17 @@ def tile_realimagfourvallinear_pa_kernel(
             [keep.tile([P, PASSES * P], U8, name="a_scales%d_%d" % (tok, op), align_bytes=64) for op in range(3)]
             for tok in range(TOKEN_TILES)
         ]
-        stats = [keep.tile([P, 2 * D // BN_COLS, 6], F32, name="stats%d" % tok) for tok in range(TOKEN_TILES)]
+        stats = [keep.tile([P, BN_PARTS, 6], F32, name="stats%d" % tok) for tok in range(TOKEN_TILES)]
         z_tiles = {}
         planes = {}
         x_grouped = {}
 
         def statistics(tok, parts):
             for i in parts:
-                h, j = divmod(i, D // BN_COLS)
-                nc.vector.bn_stats(out=stats[tok][:, i, :], in_=x_raw[tok][:, h, BN_COLS * j : BN_COLS * (j + 1)])
+                stream, j = divmod(i, D // BN_COLS)
+                nc.vector.bn_stats(
+                    out=stats[tok][:, i, :], in_=x_raw[tok][:, stream, BN_COLS * j : BN_COLS * (j + 1)]
+                )
 
         def centre(tok):
             mv = small.tile([P, 2], F32)
@@ -168,12 +175,14 @@ def tile_realimagfourvallinear_pa_kernel(
             rstd = small.tile([P, 1], F32)
             nc.gpsimd.tensor_tensor(out=rstd[:], in0=var_eps[:], in1=minus_half[:], op=ALU.pow)
             for piece in range(PIECES):
-                h, g = divmod(piece, PASSES)
+                stream, g = divmod(piece, PASSES)
                 z = z_pool.tile([P, PACK, P], F32)
-                engine = nc.vector if tok == 0 and h == REAL else nc.gpsimd
+                engine = nc.vector if stream == REAL else nc.gpsimd
                 engine.tensor_scalar(
                     out=z[:].rearrange("p (u e) j -> p u e j", e=2),
-                    in0=x_raw[tok][:, h, K_PASS * g : K_PASS * (g + 1)].rearrange("p (u j e) -> p u e j", u=2, e=2),
+                    in0=x_raw[tok][:, stream, K_PASS * g : K_PASS * (g + 1)].rearrange(
+                        "p (u j e) -> p u e j", u=2, e=2
+                    ),
                     scalar1=minus_mean[:, 0:1],
                     scalar2=rstd[:, 0:1],
                     op0=ALU.add,
@@ -189,38 +198,38 @@ def tile_realimagfourvallinear_pa_kernel(
             )
 
         def normalise_piece(tok, piece):
-            h, g = divmod(piece, PASSES)
+            stream, g = divmod(piece, PASSES)
             if g == 0:
                 stream_planes = planes_pool.tile([P, PASSES, PACK, P], BF16)
-                planes[(tok, h)] = stream_planes
+                planes[(tok, stream)] = stream_planes
             z = z_tiles[(tok, piece)]
             z_t = work_psum.tile([P, PACK, P], F32, tag="work")
             for t in range(PACK):
                 nc.tensor.transpose(z_t[:, t, :], z[:, t, :], ident[:])
             for t in range(PACK):
                 u, e = divmod(t, 2)
-                c = PIECES * h + 2 * g + u
+                col = PIECES * stream + 2 * g + u
                 if tok == 0 and piece % 2 == 1:
                     nc.scalar.activation(
-                        out=planes[(tok, h)][:, g, t, :],
+                        out=planes[(tok, stream)][:, g, t, :],
                         in_=z_t[:, t, :],
                         func=ACT.Identity,
-                        scale=gb_t[:, e, c : c + 1],
-                        bias=gb_t[:, e, 16 + c : 17 + c],
+                        scale=gb_t[:, e, col : col + 1],
+                        bias=gb_t[:, e, GB_ROWS + col : GB_ROWS + col + 1],
                     )
                 else:
                     nc.vector.tensor_scalar(
-                        out=planes[(tok, h)][:, g, t, :],
+                        out=planes[(tok, stream)][:, g, t, :],
                         in0=z_t[:, t, :],
-                        scalar1=gb_t[:, e, c : c + 1],
-                        scalar2=gb_t[:, e, 16 + c : 17 + c],
+                        scalar1=gb_t[:, e, col : col + 1],
+                        scalar2=gb_t[:, e, GB_ROWS + col : GB_ROWS + col + 1],
                         op0=ALU.mult,
                         op1=ALU.add,
                     )
             if g == PASSES - 1:
                 grouped = xg_pool.tile([P, PASSES, P, PACK], BF16, align_bytes=64)
-                nc.vector.tensor_copy(out=grouped[:], in_=planes[(tok, h)][:].rearrange("p g t k -> p g k t"))
-                x_grouped[(tok, h)] = grouped
+                nc.vector.tensor_copy(out=grouped[:], in_=planes[(tok, stream)][:].rearrange("p g t k -> p g k t"))
+                x_grouped[(tok, stream)] = grouped
             if piece == PIECES - 1:
                 quantise_operand(tok, NR, x_grouped[(tok, REAL)])
                 quantise_operand(tok, NI, x_grouped[(tok, IMAG)])
@@ -260,10 +269,10 @@ def tile_realimagfourvallinear_pa_kernel(
             if half == 1:
                 y = y_pool.tile([P, ACC_COLS], F32)
                 nc.scalar.activation(out=y[:], in_=acc[part][:], func=ACT.Copy, scale=gain[part][:, 0:1])
-                first = (rnd // 2) * ACC_COLS
-                nc.sync.dma_start(out=outs[part][tok * P : (tok + 1) * P, first : first + ACC_COLS], in_=y[:])
+                first_col = (rnd // 2) * ACC_COLS
+                nc.sync.dma_start(out=outs[part][tok * P : (tok + 1) * P, first_col : first_col + ACC_COLS], in_=y[:])
 
-        statistics(0, range(8))
+        statistics(0, range(BN_PARTS))
         centre(0)
         transpose_chunk(0)
         transpose_chunk(1)
@@ -283,7 +292,7 @@ def tile_realimagfourvallinear_pa_kernel(
             if Q_LEAD + step < CHUNKS:
                 quantise_chunk(Q_LEAD + step)
             if step < STATS_STEPS:
-                share = 8 // STATS_STEPS
+                share = BN_PARTS // STATS_STEPS
                 statistics(1, range(share * step, share * (step + 1)))
             if step == STATS_STEPS - 1:
                 centre(1)

@@ -40,7 +40,8 @@ T_LEAD = 4
 Q_LEAD = T_LEAD - 1
 X1_AFTER_CHUNK = 5
 STATS_STEPS = 4
-PIECE_STEP = STATS_STEPS + 1
+CENTRE_STEP = STATS_STEPS
+PIECE_STEP = CENTRE_STEP + 1
 
 FLOPS = 4 * 2 * TOKENS * D * N_OUT
 
@@ -154,6 +155,7 @@ def tile_realimagfourvallinear_pa_kernel(
             for tok in range(TOKEN_TILES)
         ]
         stats = [keep.tile([P, BN_PARTS, 6], F32, name="stats%d" % tok) for tok in range(TOKEN_TILES)]
+        row = {}
         z_tiles = {}
         planes = {}
         x_grouped = {}
@@ -165,7 +167,7 @@ def tile_realimagfourvallinear_pa_kernel(
                     out=stats[tok][:, i, :], in_=x_raw[tok][:, stream, BN_COLS * j : BN_COLS * (j + 1)]
                 )
 
-        def centre(tok):
+        def row_scalars(tok):
             mv = small.tile([P, 2], F32)
             nc.vector.bn_aggr(out=mv[:], in_=stats[tok][:].rearrange("p c s -> p (c s)"))
             var_eps = small.tile([P, 1], F32)
@@ -174,21 +176,21 @@ def tile_realimagfourvallinear_pa_kernel(
             nc.vector.tensor_scalar(out=minus_mean[:], in0=mv[:, 0:1], scalar1=-1.0, scalar2=None, op0=ALU.mult)
             rstd = small.tile([P, 1], F32)
             nc.gpsimd.tensor_tensor(out=rstd[:], in0=var_eps[:], in1=minus_half[:], op=ALU.pow)
-            for piece in range(PIECES):
-                stream, g = divmod(piece, PASSES)
-                z = z_pool.tile([P, PACK, P], F32)
-                engine = nc.vector if stream == REAL else nc.gpsimd
-                engine.tensor_scalar(
-                    out=z[:].rearrange("p (u e) j -> p u e j", e=2),
-                    in0=x_raw[tok][:, stream, K_PASS * g : K_PASS * (g + 1)].rearrange(
-                        "p (u j e) -> p u e j", u=2, e=2
-                    ),
-                    scalar1=minus_mean[:, 0:1],
-                    scalar2=rstd[:, 0:1],
-                    op0=ALU.add,
-                    op1=ALU.mult,
-                )
-                z_tiles[(tok, piece)] = z
+            row[tok] = (minus_mean, rstd)
+
+        def centre_piece(tok, piece):
+            stream, g = divmod(piece, PASSES)
+            minus_mean, rstd = row[tok]
+            z = z_pool.tile([P, PACK, P], F32)
+            nc.vector.tensor_scalar(
+                out=z[:].rearrange("p (u e) j -> p u e j", e=2),
+                in0=x_raw[tok][:, stream, K_PASS * g : K_PASS * (g + 1)].rearrange("p (u j e) -> p u e j", u=2, e=2),
+                scalar1=minus_mean[:, 0:1],
+                scalar2=rstd[:, 0:1],
+                op0=ALU.add,
+                op1=ALU.mult,
+            )
+            z_tiles[(tok, piece)] = z
 
         def quantise_operand(tok, op, grouped):
             nc.vector.quantize_mx(
@@ -273,7 +275,9 @@ def tile_realimagfourvallinear_pa_kernel(
                 nc.sync.dma_start(out=outs[part][tok * P : (tok + 1) * P, first_col : first_col + ACC_COLS], in_=y[:])
 
         statistics(0, range(BN_PARTS))
-        centre(0)
+        row_scalars(0)
+        for piece in range(PIECES):
+            centre_piece(0, piece)
         transpose_chunk(0)
         transpose_chunk(1)
         quantise_chunk(0)
@@ -295,7 +299,9 @@ def tile_realimagfourvallinear_pa_kernel(
                 share = BN_PARTS // STATS_STEPS
                 statistics(1, range(share * step, share * (step + 1)))
             if step == STATS_STEPS - 1:
-                centre(1)
+                row_scalars(1)
+            if CENTRE_STEP <= step < CENTRE_STEP + PIECES:
+                centre_piece(1, step - CENTRE_STEP)
             if PIECE_STEP <= step < PIECE_STEP + PIECES:
                 normalise_piece(1, step - PIECE_STEP)
             multiply(0, step)

@@ -26,12 +26,14 @@ K_PASS = P * PACK
 PASSES = D // K_PASS
 PIECES = 2 * PASSES
 N_CHUNK = 256
+ROW_BLOCKS = N_CHUNK // P
 ROUNDS = N_OUT // N_CHUNK
 CHUNKS = 2 * ROUNDS
 STEPS = 2 * ROUNDS
 ACC_COLS = 2 * N_CHUNK
 BN_COLS = 512
-BN_PARTS = 2 * D // BN_COLS
+BN_CALLS = 2 * D // BN_COLS
+BN_VALUES = 6
 GB_COLS = 2 * P
 GB_ROWS = 2 * D // GB_COLS
 
@@ -70,8 +72,8 @@ def tile_realimagfourvallinear_pa_kernel(
 
         gb_raw = const.tile([P, GB_COLS], BF16)
         nc.vector.memset(gb_raw[:], 0.0)
-        nc.sync.dma_start(out=gb_raw[0:GB_ROWS, :], in_=gamma.rearrange("(c k) -> c k", k=GB_COLS))
-        nc.sync.dma_start(out=gb_raw[GB_ROWS : 2 * GB_ROWS, :], in_=beta.rearrange("(c k) -> c k", k=GB_COLS))
+        nc.sync.dma_start(out=gb_raw[0:GB_ROWS, :], in_=gamma.rearrange("(row k) -> row k", k=GB_COLS))
+        nc.sync.dma_start(out=gb_raw[GB_ROWS : 2 * GB_ROWS, :], in_=beta.rearrange("(row k) -> row k", k=GB_COLS))
         gain_bf = [const.tile([P, 1], BF16, name="gain_bf%d" % part) for part in range(2)]
         nc.scalar.dma_start(out=gain_bf[REAL][:], in_=s_re.partition_broadcast(P))
         nc.scalar.dma_start(out=gain_bf[IMAG][:], in_=s_im.partition_broadcast(P))
@@ -88,7 +90,7 @@ def tile_realimagfourvallinear_pa_kernel(
 
         def load_chunk(c):
             rnd, matrix = divmod(c, 2)
-            raw = w_pool.tile([P, 2, D], BF16)
+            raw = w_pool.tile([P, ROW_BLOCKS, D], BF16)
             rows = weights[matrix][rnd * N_CHUNK : (rnd + 1) * N_CHUNK, :]
             nc.sync.dma_start(out=raw[:], in_=rows.rearrange("(r p) k -> p r k", p=P))
             w_raw[c] = raw
@@ -128,7 +130,7 @@ def tile_realimagfourvallinear_pa_kernel(
             grouped_words = grouped[:].bitcast(F32)
             for g in range(PASSES):
                 bank = wt_psum.tile([P, 2, N_CHUNK], F32)
-                for r in range(2):
+                for r in range(ROW_BLOCKS):
                     for u in range(2):
                         first_word = 2 * P * g + P * u
                         nc.tensor.transpose(
@@ -154,22 +156,22 @@ def tile_realimagfourvallinear_pa_kernel(
             [keep.tile([P, PASSES * P], U8, name="a_scales%d_%d" % (tok, op), align_bytes=64) for op in range(3)]
             for tok in range(TOKEN_TILES)
         ]
-        stats = [keep.tile([P, BN_PARTS, 6], F32, name="stats%d" % tok) for tok in range(TOKEN_TILES)]
+        stats = [keep.tile([P, BN_CALLS, BN_VALUES], F32, name="stats%d" % tok) for tok in range(TOKEN_TILES)]
         row = {}
         z_tiles = {}
         planes = {}
         x_grouped = {}
 
-        def statistics(tok, parts):
-            for i in parts:
-                stream, j = divmod(i, D // BN_COLS)
+        def statistics(tok, calls):
+            for call in calls:
+                stream, block = divmod(call, D // BN_COLS)
                 nc.vector.bn_stats(
-                    out=stats[tok][:, i, :], in_=x_raw[tok][:, stream, BN_COLS * j : BN_COLS * (j + 1)]
+                    out=stats[tok][:, call, :], in_=x_raw[tok][:, stream, BN_COLS * block : BN_COLS * (block + 1)]
                 )
 
         def row_scalars(tok):
             mv = small.tile([P, 2], F32)
-            nc.vector.bn_aggr(out=mv[:], in_=stats[tok][:].rearrange("p c s -> p (c s)"))
+            nc.vector.bn_aggr(out=mv[:], in_=stats[tok][:].rearrange("p call v -> p (call v)"))
             var_eps = small.tile([P, 1], F32)
             nc.vector.tensor_scalar(out=var_eps[:], in0=mv[:, 1:2], scalar1=EPS, scalar2=None, op0=ALU.add)
             minus_mean = small.tile([P, 1], F32)
@@ -182,7 +184,8 @@ def tile_realimagfourvallinear_pa_kernel(
             stream, g = divmod(piece, PASSES)
             minus_mean, rstd = row[tok]
             z = z_pool.tile([P, PACK, P], F32)
-            nc.vector.tensor_scalar(
+            engine = nc.vector if stream == REAL else nc.gpsimd
+            engine.tensor_scalar(
                 out=z[:].rearrange("p (u e) j -> p u e j", e=2),
                 in0=x_raw[tok][:, stream, K_PASS * g : K_PASS * (g + 1)].rearrange("p (u j e) -> p u e j", u=2, e=2),
                 scalar1=minus_mean[:, 0:1],
@@ -196,7 +199,7 @@ def tile_realimagfourvallinear_pa_kernel(
             nc.vector.quantize_mx(
                 out=a_codes[tok][op][:].bitcast(FP8X4),
                 scales=a_scales[tok][op][:],
-                in_=grouped[:].rearrange("p g k t -> p (g k t)"),
+                in_=grouped[:].rearrange("p g i t -> p (g i t)"),
             )
 
         def normalise_piece(tok, piece):
@@ -210,7 +213,7 @@ def tile_realimagfourvallinear_pa_kernel(
                 nc.tensor.transpose(z_t[:, t, :], z[:, t, :], ident[:])
             for t in range(PACK):
                 u, e = divmod(t, 2)
-                col = PIECES * stream + 2 * g + u
+                col = (D // GB_COLS) * stream + 2 * g + u
                 if tok == 0 and piece % 2 == 1:
                     nc.scalar.activation(
                         out=planes[(tok, stream)][:, g, t, :],
@@ -230,15 +233,15 @@ def tile_realimagfourvallinear_pa_kernel(
                     )
             if g == PASSES - 1:
                 grouped = xg_pool.tile([P, PASSES, P, PACK], BF16, align_bytes=64)
-                nc.vector.tensor_copy(out=grouped[:], in_=planes[(tok, stream)][:].rearrange("p g t k -> p g k t"))
+                nc.vector.tensor_copy(out=grouped[:], in_=planes[(tok, stream)][:].rearrange("p g t i -> p g i t"))
                 x_grouped[(tok, stream)] = grouped
             if piece == PIECES - 1:
                 quantise_operand(tok, NR, x_grouped[(tok, REAL)])
                 quantise_operand(tok, NI, x_grouped[(tok, IMAG)])
                 negated = xg_pool.tile([P, PASSES, P, PACK], BF16, align_bytes=64, tag="grouped")
                 nc.vector.tensor_scalar(
-                    out=negated[:].rearrange("p g k t -> p (g k t)"),
-                    in0=x_grouped[(tok, IMAG)][:].rearrange("p g k t -> p (g k t)"),
+                    out=negated[:].rearrange("p g i t -> p (g i t)"),
+                    in0=x_grouped[(tok, IMAG)][:].rearrange("p g i t -> p (g i t)"),
                     scalar1=-1.0,
                     scalar2=None,
                     op0=ALU.mult,
@@ -256,7 +259,7 @@ def tile_realimagfourvallinear_pa_kernel(
                 acc[part] = bank
             cols = acc[part][:, half * N_CHUNK : (half + 1) * N_CHUNK]
             pairs = ((NR, REAL), (NEG_NI, IMAG)) if part == REAL else ((NR, IMAG), (NI, REAL))
-            for i, (op, matrix) in enumerate(pairs):
+            for product, (op, matrix) in enumerate(pairs):
                 c = 2 * rnd + matrix
                 for g in range(PASSES):
                     nc.tensor.matmul_mx(
@@ -265,8 +268,8 @@ def tile_realimagfourvallinear_pa_kernel(
                         lhsT_scale=a_scales[tok][op][:, g * P : (g + 1) * P],
                         rhs=w_codes[c][:, g * N_CHUNK : (g + 1) * N_CHUNK].bitcast(FP8X4),
                         rhs_scale=w_scales[c][:, g * N_CHUNK : (g + 1) * N_CHUNK],
-                        start=(i == 0 and g == 0),
-                        stop=(i == 1 and g == PASSES - 1),
+                        start=(product == 0 and g == 0),
+                        stop=(product == 1 and g == PASSES - 1),
                     )
             if half == 1:
                 y = y_pool.tile([P, ACC_COLS], F32)
@@ -274,7 +277,7 @@ def tile_realimagfourvallinear_pa_kernel(
                 first_col = (rnd // 2) * ACC_COLS
                 nc.sync.dma_start(out=outs[part][tok * P : (tok + 1) * P, first_col : first_col + ACC_COLS], in_=y[:])
 
-        statistics(0, range(BN_PARTS))
+        statistics(0, range(BN_CALLS))
         row_scalars(0)
         for piece in range(PIECES):
             centre_piece(0, piece)
@@ -296,7 +299,7 @@ def tile_realimagfourvallinear_pa_kernel(
             if Q_LEAD + step < CHUNKS:
                 quantise_chunk(Q_LEAD + step)
             if step < STATS_STEPS:
-                share = BN_PARTS // STATS_STEPS
+                share = BN_CALLS // STATS_STEPS
                 statistics(1, range(share * step, share * (step + 1)))
             if step == STATS_STEPS - 1:
                 row_scalars(1)

from contextlib import ExitStack

import concourse.mybir as mybir
from concourse.masks import make_identity

F32 = mybir.dt.float32
BF16 = mybir.dt.bfloat16
U32 = mybir.dt.uint32
U8 = mybir.dt.uint8
FP8X4 = mybir.dt.float8_e4m3fn_x4
ALU = mybir.AluOpType
ACT = mybir.ActivationFunctionType

P = 128
TOKENS = 256
TOKEN_TILES = TOKENS // P
D = 2048
N_OUT = 2048
EPS = 1e-6

REAL, IMAG = 0, 1
NR, NI, NEG_NI = 0, 1, 2

PACK = 4
K_PASS = P * PACK
PASSES = D // K_PASS
PIECES = 2 * PASSES
N_CHUNK = 256
ROW_BLOCKS = N_CHUNK // P
ROUNDS = N_OUT // N_CHUNK
CHUNKS = 2 * ROUNDS
STEPS = 2 * ROUNDS
ACC_COLS = 2 * N_CHUNK
BN_COLS = 512
BN_CALLS = 2 * D // BN_COLS
BN_VALUES = 6
GB_COLS = 2 * P
GB_ROWS = 2 * D // GB_COLS

W_BUFS = 5
T_LEAD = 4
Q_LEAD = T_LEAD - 1
X1_AFTER_CHUNK = 5
STATS_STEPS = 4
CENTRE_STEP = STATS_STEPS
PIECE_STEP = CENTRE_STEP + 1

FLOPS = 4 * 2 * TOKENS * D * N_OUT


def tile_realimagfourvallinear_pa_kernel(
    tc, x_real, x_imag, qw_re, qw_im, gamma, beta, s_re, s_im, out_0, out_1
):
    nc = tc.nc
    x_streams = (x_real.flatten_outer_dims(), x_imag.flatten_outer_dims())
    weights = (qw_re, qw_im)
    outs = (out_0.flatten_outer_dims(), out_1.flatten_outer_dims())

    with ExitStack() as ctx:
        const = ctx.enter_context(tc.tile_pool(name="const", bufs=1))
        keep = ctx.enter_context(tc.tile_pool(name="keep", bufs=1))
        small = ctx.enter_context(tc.tile_pool(name="small", bufs=2))
        w_pool = ctx.enter_context(tc.tile_pool(name="w_pool", bufs=W_BUFS))
        wg_pool = ctx.enter_context(tc.tile_pool(name="wg_pool", bufs=3))
        z_pool = ctx.enter_context(tc.tile_pool(name="z_pool", bufs=PIECES))
        planes_pool = ctx.enter_context(tc.tile_pool(name="planes_pool", bufs=2))
        xg_pool = ctx.enter_context(tc.tile_pool(name="xg_pool", bufs=3))
        y_pool = ctx.enter_context(tc.tile_pool(name="y_pool", bufs=4))
        wt_psum = ctx.enter_context(tc.psum_pool(name="wt_psum", bufs=4))
        work_psum = ctx.enter_context(tc.psum_pool(name="work_psum", bufs=4))
        ctx.enter_context(tc.manual_schedule())

        gb_raw = const.tile([P, GB_COLS], BF16)
        nc.vector.memset(gb_raw[:], 0.0)
        nc.sync.dma_start(out=gb_raw[0:GB_ROWS, :], in_=gamma.rearrange("(row k) -> row k", k=GB_COLS))
        nc.sync.dma_start(out=gb_raw[GB_ROWS : 2 * GB_ROWS, :], in_=beta.rearrange("(row k) -> row k", k=GB_COLS))
        gain_bf = [const.tile([P, 1], BF16, name="gain_bf%d" % part) for part in range(2)]
        nc.scalar.dma_start(out=gain_bf[REAL][:], in_=s_re.partition_broadcast(P))
        nc.scalar.dma_start(out=gain_bf[IMAG][:], in_=s_im.partition_broadcast(P))

        x_raw = [keep.tile([P, 2, D], BF16, name="x_raw%d" % tok) for tok in range(TOKEN_TILES)]

        def load_x(tok):
            for stream in range(2):
                nc.sync.dma_start(
                    out=x_raw[tok][:, stream, :], in_=x_streams[stream][tok * P : (tok + 1) * P, :]
                )

        w_raw = {}

        def load_chunk(c):
            rnd, matrix = divmod(c, 2)
            raw = w_pool.tile([P, ROW_BLOCKS, D], BF16)
            rows = weights[matrix][rnd * N_CHUNK : (rnd + 1) * N_CHUNK, :]
            nc.sync.dma_start(out=raw[:], in_=rows.rearrange("(r p) k -> p r k", p=P))
            w_raw[c] = raw
            if c == X1_AFTER_CHUNK:
                load_x(1)

        load_x(0)
        for c in range(W_BUFS):
            load_chunk(c)

        ident = const.tile([P, P], F32)
        make_identity(nc, ident[:])
        minus_half = const.tile([P, 1], F32)
        nc.gpsimd.memset(minus_half[:], -0.5)
        gb_f32 = const.tile([P, 2, P], F32)
        nc.gpsimd.tensor_copy(out=gb_f32[:], in_=gb_raw[:].rearrange("p (j e) -> p e j", e=2))
        gb_ps = work_psum.tile([P, 2, P], F32, tag="work")
        for e in range(2):
            nc.tensor.transpose(gb_ps[:, e, :], gb_f32[:, e, :], ident[:])
        gb_t = const.tile([P, 2, 2 * GB_ROWS], F32)
        nc.scalar.copy(out=gb_t[:], in_=gb_ps[:, :, 0 : 2 * GB_ROWS])
        gain = [const.tile([P, 1], F32, name="gain%d" % part) for part in range(2)]
        for part in range(2):
            nc.gpsimd.tensor_copy(out=gain[part][:], in_=gain_bf[part][:])

        w_codes = [
            keep.tile([P, PASSES * N_CHUNK], U32, name="w_codes%d" % c, align_bytes=64) for c in range(CHUNKS)
        ]
        w_scales = [
            keep.tile([P, PASSES * N_CHUNK], U8, name="w_scales%d" % c, align_bytes=64) for c in range(CHUNKS)
        ]
        w_grouped = {}

        def transpose_chunk(c):
            words = w_raw[c][:].bitcast(F32)
            grouped = wg_pool.tile([P, PASSES, N_CHUNK, PACK], BF16, align_bytes=64)
            grouped_words = grouped[:].bitcast(F32)
            for g in range(PASSES):
                bank = wt_psum.tile([P, 2, N_CHUNK], F32)
                for r in range(ROW_BLOCKS):
                    for u in range(2):
                        first_word = 2 * P * g + P * u
                        nc.tensor.transpose(
                            bank[:, u, r * P : (r + 1) * P], words[:, r, first_word : first_word + P], ident[:]
                        )
                nc.scalar.copy(out=grouped_words[:, g, :, :], in_=bank[:].rearrange("p u n -> p n u"))
            w_grouped[c] = grouped
            if c + W_BUFS < CHUNKS:
                load_chunk(c + W_BUFS)

        def quantise_chunk(c):
            nc.vector.quantize_mx(
                out=w_codes[c][:].bitcast(FP8X4),
                scales=w_scales[c][:],
                in_=w_grouped[c][:].rearrange("p g n t -> p (g n t)"),
            )

        a_codes = [
            [keep.tile([P, PASSES * P], U32, name="a_codes%d_%d" % (tok, op), align_bytes=64) for op in range(3)]
            for tok in range(TOKEN_TILES)
        ]
        a_scales = [
            [keep.tile([P, PASSES * P], U8, name="a_scales%d_%d" % (tok, op), align_bytes=64) for op in range(3)]
            for tok in range(TOKEN_TILES)
        ]
        stats = [keep.tile([P, BN_CALLS, BN_VALUES], F32, name="stats%d" % tok) for tok in range(TOKEN_TILES)]
        row = {}
        z_tiles = {}
        planes = {}
        x_grouped = {}

        def statistics(tok, calls):
            for call in calls:
                stream, block = divmod(call, D // BN_COLS)
                nc.vector.bn_stats(
                    out=stats[tok][:, call, :], in_=x_raw[tok][:, stream, BN_COLS * block : BN_COLS * (block + 1)]
                )

        def row_scalars(tok):
            mv = small.tile([P, 2], F32)
            nc.vector.bn_aggr(out=mv[:], in_=stats[tok][:].rearrange("p call v -> p (call v)"))
            var_eps = small.tile([P, 1], F32)
            nc.vector.tensor_scalar(out=var_eps[:], in0=mv[:, 1:2], scalar1=EPS, scalar2=None, op0=ALU.add)
            minus_mean = small.tile([P, 1], F32)
            nc.vector.tensor_scalar(out=minus_mean[:], in0=mv[:, 0:1], scalar1=-1.0, scalar2=None, op0=ALU.mult)
            rstd = small.tile([P, 1], F32)
            nc.gpsimd.tensor_tensor(out=rstd[:], in0=var_eps[:], in1=minus_half[:], op=ALU.pow)
            row[tok] = (minus_mean, rstd)

        def centre_piece(tok, piece):
            stream, g = divmod(piece, PASSES)
            minus_mean, rstd = row[tok]
            z = z_pool.tile([P, PACK, P], F32)
            engine = nc.vector if stream == REAL else nc.gpsimd
            engine.tensor_scalar(
                out=z[:].rearrange("p (u e) j -> p u e j", e=2),
                in0=x_raw[tok][:, stream, K_PASS * g : K_PASS * (g + 1)].rearrange("p (u j e) -> p u e j", u=2, e=2),
                scalar1=minus_mean[:, 0:1],
                scalar2=rstd[:, 0:1],
                op0=ALU.add,
                op1=ALU.mult,
            )
            z_tiles[(tok, piece)] = z

        def quantise_operand(tok, op, grouped):
            nc.vector.quantize_mx(
                out=a_codes[tok][op][:].bitcast(FP8X4),
                scales=a_scales[tok][op][:],
                in_=grouped[:].rearrange("p g i t -> p (g i t)"),
            )

        def normalise_piece(tok, piece):
            stream, g = divmod(piece, PASSES)
            if g == 0:
                stream_planes = planes_pool.tile([P, PASSES, PACK, P], BF16)
                planes[(tok, stream)] = stream_planes
            z = z_tiles[(tok, piece)]
            z_t = work_psum.tile([P, PACK, P], F32, tag="work")
            for t in range(PACK):
                nc.tensor.transpose(z_t[:, t, :], z[:, t, :], ident[:])
            for t in range(PACK):
                u, e = divmod(t, 2)
                col = (D // GB_COLS) * stream + 2 * g + u
                if tok == 0 and piece % 2 == 1:
                    nc.scalar.activation(
                        out=planes[(tok, stream)][:, g, t, :],
                        in_=z_t[:, t, :],
                        func=ACT.Identity,
                        scale=gb_t[:, e, col : col + 1],
                        bias=gb_t[:, e, GB_ROWS + col : GB_ROWS + col + 1],
                    )
                else:
                    nc.vector.tensor_scalar(
                        out=planes[(tok, stream)][:, g, t, :],
                        in0=z_t[:, t, :],
                        scalar1=gb_t[:, e, col : col + 1],
                        scalar2=gb_t[:, e, GB_ROWS + col : GB_ROWS + col + 1],
                        op0=ALU.mult,
                        op1=ALU.add,
                    )
            if g == PASSES - 1:
                grouped = xg_pool.tile([P, PASSES, P, PACK], BF16, align_bytes=64)
                nc.vector.tensor_copy(out=grouped[:], in_=planes[(tok, stream)][:].rearrange("p g t i -> p g i t"))
                x_grouped[(tok, stream)] = grouped
            if piece == PIECES - 1:
                quantise_operand(tok, NR, x_grouped[(tok, REAL)])
                quantise_operand(tok, NI, x_grouped[(tok, IMAG)])
                negated = xg_pool.tile([P, PASSES, P, PACK], BF16, align_bytes=64, tag="grouped")
                nc.vector.tensor_scalar(
                    out=negated[:].rearrange("p g i t -> p (g i t)"),
                    in0=x_grouped[(tok, IMAG)][:].rearrange("p g i t -> p (g i t)"),
                    scalar1=-1.0,
                    scalar2=None,
                    op0=ALU.mult,
                )
                quantise_operand(tok, NEG_NI, negated)

        acc = {}

        def multiply(tok, step):
            rnd = step // 2
            part = (IMAG, REAL)[step % 2]
            half = rnd % 2
            if half == 0:
                bank = work_psum.tile([P, ACC_COLS], F32, tag="work")
                acc[part] = bank
            cols = acc[part][:, half * N_CHUNK : (half + 1) * N_CHUNK]
            pairs = ((NR, REAL), (NEG_NI, IMAG)) if part == REAL else ((NR, IMAG), (NI, REAL))
            for product, (op, matrix) in enumerate(pairs):
                c = 2 * rnd + matrix
                for g in range(PASSES):
                    nc.tensor.matmul_mx(
                        out=cols,
                        lhsT=a_codes[tok][op][:, g * P : (g + 1) * P].bitcast(FP8X4),
                        lhsT_scale=a_scales[tok][op][:, g * P : (g + 1) * P],
                        rhs=w_codes[c][:, g * N_CHUNK : (g + 1) * N_CHUNK].bitcast(FP8X4),
                        rhs_scale=w_scales[c][:, g * N_CHUNK : (g + 1) * N_CHUNK],
                        start=(product == 0 and g == 0),
                        stop=(product == 1 and g == PASSES - 1),
                    )
            if half == 1:
                y = y_pool.tile([P, ACC_COLS], F32)
                nc.scalar.activation(out=y[:], in_=acc[part][:], func=ACT.Copy, scale=gain[part][:, 0:1])
                first_col = (rnd // 2) * ACC_COLS
                nc.sync.dma_start(out=outs[part][tok * P : (tok + 1) * P, first_col : first_col + ACC_COLS], in_=y[:])

        statistics(0, range(BN_CALLS))
        row_scalars(0)
        for piece in range(PIECES):
            centre_piece(0, piece)
        transpose_chunk(0)
        transpose_chunk(1)
        quantise_chunk(0)
        for piece in range(PASSES):
            normalise_piece(0, piece)
        transpose_chunk(2)
        quantise_chunk(1)
        for piece in range(PASSES, PIECES):
            normalise_piece(0, piece)
        transpose_chunk(3)
        quantise_chunk(2)

        for step in range(STEPS):
            if T_LEAD + step < CHUNKS:
                transpose_chunk(T_LEAD + step)
            if Q_LEAD + step < CHUNKS:
                quantise_chunk(Q_LEAD + step)
            if step < STATS_STEPS:
                share = BN_CALLS // STATS_STEPS
                statistics(1, range(share * step, share * (step + 1)))
            if step == STATS_STEPS - 1:
                row_scalars(1)
            if CENTRE_STEP <= step < CENTRE_STEP + PIECES:
                centre_piece(1, step - CENTRE_STEP)
            if PIECE_STEP <= step < PIECE_STEP + PIECES:
                normalise_piece(1, step - PIECE_STEP)
            multiply(0, step)

        for step in range(STEPS):
            multiply(1, step)
